import numpy as np
import ml_dtypes

BF16 = ml_dtypes.bfloat16


def bf(x):
    return np.asarray(x, np.float32).astype(BF16)


def f32(x):
    return np.asarray(x, np.float32)


def f64(x):
    return np.asarray(x).astype(np.float64)


def striped(idx):
    return np.tile(idx.reshape(-1, 16).T, (8, 1))


C, S, N, P = 256, 512, 128, 16


def setup_inputs():
    return {"base": f32(np.random.standard_normal((C, S))), "v": f32(np.random.standard_normal((C, N * P))), "bv": f32(0.1 * np.random.standard_normal((C, 1))), "q": f32(np.random.standard_normal((C, N))), "offs": striped(np.random.permutation(S)[:N])}


def reference(base, v, bv, q, offs):
    idx = offs[:16].T.reshape(-1)
    att = f64(v).reshape(C, N, P).mean(axis=-1) + f64(bv)
    out = f64(base).copy()
    out[:, idx] = att + f64(q)
    return out

@@ -1,0 +1,52 @@
+import concourse.mybir as mybir
+
+F32 = mybir.dt.float32
+U16 = mybir.dt.uint16
+ADD = mybir.AluOpType.add
+MULT = mybir.AluOpType.mult
+X = mybir.AxisListType.X
+
+CHANNELS, PLACES, FRUSTUMS, POINTS = 256, 512, 128, 16
+P = 128
+BLOCKS = CHANNELS // P
+CHUNKS = 4
+CHUNK = FRUSTUMS // CHUNKS
+
+
+def tile_transformerfrustumencoder_kernel(tc, base, v, bv, q, offs, out):
+    nc = tc.nc
+    with (
+        tc.tile_pool(name="held", bufs=1) as held,
+        tc.tile_pool(name="per_block", bufs=BLOCKS) as per_block,
+        tc.tile_pool(name="per_chunk", bufs=BLOCKS * CHUNKS) as per_chunk,
+    ):
+        offsets = held.tile([P, FRUSTUMS // 16], U16, name="offsets")
+        nc.sync.dma_start(offsets[:], offs)
+
+        for b in range(BLOCKS):
+            rows = slice(b * P, (b + 1) * P)
+
+            image = per_block.tile([P, PLACES], F32, name="image")
+            nc.sync.dma_start(image[:], base[rows, :])
+            query = per_block.tile([P, FRUSTUMS], F32, name="query")
+            nc.sync.dma_start(query[:], q[rows, :])
+            bias = per_block.tile([P, 1], F32, name="bias")
+            nc.sync.dma_start(bias[:], bv[rows, :])
+
+            sums = per_block.tile([P, FRUSTUMS], F32, name="sums")
+            for k in range(CHUNKS):
+                first = k * CHUNK
+                points = per_chunk.tile([P, CHUNK, POINTS], F32, name="points")
+                nc.sync.dma_start(
+                    points[:],
+                    v[rows, first * POINTS : (first + CHUNK) * POINTS].rearrange(
+                        "c (j p) -> c j p", p=POINTS
+                    ),
+                )
+                nc.vector.tensor_reduce(sums[:, first : first + CHUNK], points[:], X, ADD)
+
+            pooled = per_block.tile([P, FRUSTUMS], F32, name="pooled")
+            nc.vector.tensor_scalar(pooled[:], sums[:], 1.0 / POINTS, bias[:], MULT, ADD)
+
+            nc.vector.tensor_tensor(image[:].indirect(offsets[:]), pooled[:], query[:], ADD)
+            nc.scalar.dma_start(out[rows, :], image[:])

@@ -23,30 +23,34 @@ def tile_transformerfrustumencoder_kernel(tc, base, v, bv, q, offs, out):
         offsets = held.tile([P, FRUSTUMS // 16], U16, name="offsets")
         nc.sync.dma_start(offsets[:], offs)
 
+        points = {}
         for b in range(BLOCKS):
-            rows = slice(b * P, (b + 1) * P)
-
-            image = per_block.tile([P, PLACES], F32, name="image")
-            nc.sync.dma_start(image[:], base[rows, :])
-            query = per_block.tile([P, FRUSTUMS], F32, name="query")
-            nc.sync.dma_start(query[:], q[rows, :])
-            bias = per_block.tile([P, 1], F32, name="bias")
-            nc.sync.dma_start(bias[:], bv[rows, :])
-
-            sums = per_block.tile([P, FRUSTUMS], F32, name="sums")
             for k in range(CHUNKS):
-                first = k * CHUNK
-                points = per_chunk.tile([P, CHUNK, POINTS], F32, name="points")
+                points[b, k] = per_chunk.tile([P, CHUNK, POINTS], F32, name="points")
                 nc.sync.dma_start(
-                    points[:],
-                    v[rows, first * POINTS : (first + CHUNK) * POINTS].rearrange(
+                    points[b, k][:],
+                    v[b * P : (b + 1) * P, k * CHUNK * POINTS : (k + 1) * CHUNK * POINTS].rearrange(
                         "c (j p) -> c j p", p=POINTS
                     ),
                 )
-                nc.vector.tensor_reduce(sums[:, first : first + CHUNK], points[:], X, ADD)
+        image, query, bias = {}, {}, {}
+        for b in range(BLOCKS):
+            rows = slice(b * P, (b + 1) * P)
+            bias[b] = per_block.tile([P, 1], F32, name="bias")
+            nc.sync.dma_start(bias[b][:], bv[rows, :])
+            query[b] = per_block.tile([P, FRUSTUMS], F32, name="query")
+            nc.sync.dma_start(query[b][:], q[rows, :])
+            image[b] = per_block.tile([P, PLACES], F32, name="image")
+            nc.sync.dma_start(image[b][:], base[rows, :])
 
+        sums = {}
+        for b in range(BLOCKS):
+            sums[b] = per_block.tile([P, FRUSTUMS], F32, name="sums")
+            for k in range(CHUNKS):
+                nc.vector.tensor_reduce(sums[b][:, k * CHUNK : (k + 1) * CHUNK], points[b, k][:], X, ADD)
+
+        for b in range(BLOCKS):
             pooled = per_block.tile([P, FRUSTUMS], F32, name="pooled")
-            nc.vector.tensor_scalar(pooled[:], sums[:], 1.0 / POINTS, bias[:], MULT, ADD)
-
-            nc.vector.tensor_tensor(image[:].indirect(offsets[:]), pooled[:], query[:], ADD)
-            nc.scalar.dma_start(out[rows, :], image[:])
+            nc.vector.tensor_scalar(pooled[:], sums[b][:], 1.0 / POINTS, bias[b][:], MULT, ADD)
+            nc.vector.tensor_tensor(image[b][:].indirect(offsets[:]), pooled[:], query[b][:], ADD)
+            nc.scalar.dma_start(out[b * P : (b + 1) * P, :], image[b][:])

@@ -20,9 +20,6 @@ def tile_transformerfrustumencoder_kernel(tc, base, v, bv, q, offs, out):
         tc.tile_pool(name="per_block", bufs=BLOCKS) as per_block,
         tc.tile_pool(name="per_chunk", bufs=BLOCKS * CHUNKS) as per_chunk,
     ):
-        offsets = held.tile([P, FRUSTUMS // 16], U16, name="offsets")
-        nc.sync.dma_start(offsets[:], offs)
-
         points = {}
         for b in range(BLOCKS):
             for k in range(CHUNKS):
@@ -33,24 +30,28 @@ def tile_transformerfrustumencoder_kernel(tc, base, v, bv, q, offs, out):
                         "c (j p) -> c j p", p=POINTS
                     ),
                 )
-        image, query, bias = {}, {}, {}
+        offsets = held.tile([P, FRUSTUMS // 16], U16, name="offsets")
+        nc.sync.dma_start(offsets[:], offs)
+        image = {}
         for b in range(BLOCKS):
-            rows = slice(b * P, (b + 1) * P)
-            bias[b] = per_block.tile([P, 1], F32, name="bias")
-            nc.sync.dma_start(bias[b][:], bv[rows, :])
-            query[b] = per_block.tile([P, FRUSTUMS], F32, name="query")
-            nc.sync.dma_start(query[b][:], q[rows, :])
             image[b] = per_block.tile([P, PLACES], F32, name="image")
-            nc.sync.dma_start(image[b][:], base[rows, :])
+            nc.sync.dma_start(image[b][:], base[b * P : (b + 1) * P, :])
 
-        sums = {}
+        query, bias = {}, {}
         for b in range(BLOCKS):
-            sums[b] = per_block.tile([P, FRUSTUMS], F32, name="sums")
+            bias[b] = per_block.tile([P, 1], F32, name="bias")
+            nc.scalar.dma_start(bias[b][:], bv[b * P : (b + 1) * P, :])
+            query[b] = per_block.tile([P, FRUSTUMS], F32, name="query")
+            nc.scalar.dma_start(query[b][:], q[b * P : (b + 1) * P, :])
+
+        pooled = {}
+        for b in range(BLOCKS):
+            sums = per_block.tile([P, FRUSTUMS], F32, name="sums")
             for k in range(CHUNKS):
-                nc.vector.tensor_reduce(sums[b][:, k * CHUNK : (k + 1) * CHUNK], points[b, k][:], X, ADD)
+                nc.vector.tensor_reduce(sums[:, k * CHUNK : (k + 1) * CHUNK], points[b, k][:], X, ADD)
+            pooled[b] = per_block.tile([P, FRUSTUMS], F32, name="pooled")
+            nc.vector.tensor_scalar(pooled[b][:], sums[:], 1.0 / POINTS, bias[b][:], MULT, ADD)
 
         for b in range(BLOCKS):
-            pooled = per_block.tile([P, FRUSTUMS], F32, name="pooled")
-            nc.vector.tensor_scalar(pooled[:], sums[b][:], 1.0 / POINTS, bias[b][:], MULT, ADD)
-            nc.vector.tensor_tensor(image[b][:].indirect(offsets[:]), pooled[:], query[b][:], ADD)
+            nc.vector.tensor_tensor(image[b][:].indirect(offsets[:]), pooled[b][:], query[b][:], ADD)
             nc.scalar.dma_start(out[b * P : (b + 1) * P, :], image[b][:])

@@ -3,7 +3,7 @@ import concourse.mybir as mybir
 F32 = mybir.dt.float32
 U16 = mybir.dt.uint16
 ADD = mybir.AluOpType.add
-MULT = mybir.AluOpType.mult
+IDENTITY = mybir.ActivationFunctionType.Identity
 X = mybir.AxisListType.X
 
 CHANNELS, PLACES, FRUSTUMS, POINTS = 256, 512, 128, 16
@@ -50,7 +50,7 @@ def tile_transformerfrustumencoder_kernel(tc, base, v, bv, q, offs, out):
             for k in range(CHUNKS):
                 nc.vector.tensor_reduce(sums[:, k * CHUNK : (k + 1) * CHUNK], points[b, k][:], X, ADD)
             pooled[b] = per_block.tile([P, FRUSTUMS], F32, name="pooled")
-            nc.vector.tensor_scalar(pooled[b][:], sums[:], 1.0 / POINTS, bias[b][:], MULT, ADD)
+            nc.scalar.activation(pooled[b][:], sums[:], IDENTITY, bias=bias[b][:], scale=1.0 / POINTS)
 
         for b in range(BLOCKS):
             nc.vector.tensor_tensor(image[b][:].indirect(offsets[:]), pooled[b][:], query[b][:], ADD)

@@ -8,50 +8,46 @@ X = mybir.AxisListType.X
 
 CHANNELS, PLACES, FRUSTUMS, POINTS = 256, 512, 128, 16
 P = 128
-BLOCKS = CHANNELS // P
+HALVES = CHANNELS // P
 CHUNKS = 4
 CHUNK = FRUSTUMS // CHUNKS
 
 
 def tile_transformerfrustumencoder_kernel(tc, base, v, bv, q, offs, out):
     nc = tc.nc
+    base_by_half = base.rearrange("(c2 h) s -> c2 h s", h=HALVES)
+    out_by_half = out.rearrange("(c2 h) s -> c2 h s", h=HALVES)
+    v_by_half = v.rearrange("(c2 h) (j p) -> c2 h j p", h=HALVES, p=POINTS)
     with (
         tc.tile_pool(name="held", bufs=1) as held,
-        tc.tile_pool(name="per_block", bufs=BLOCKS) as per_block,
-        tc.tile_pool(name="per_chunk", bufs=BLOCKS * CHUNKS) as per_chunk,
+        tc.tile_pool(name="per_half", bufs=HALVES) as per_half,
+        tc.tile_pool(name="per_chunk", bufs=HALVES * CHUNKS) as per_chunk,
     ):
         points = {}
-        for b in range(BLOCKS):
+        for h in range(HALVES):
             for k in range(CHUNKS):
-                points[b, k] = per_chunk.tile([P, CHUNK, POINTS], F32, name="points")
-                nc.sync.dma_start(
-                    points[b, k][:],
-                    v[b * P : (b + 1) * P, k * CHUNK * POINTS : (k + 1) * CHUNK * POINTS].rearrange(
-                        "c (j p) -> c j p", p=POINTS
-                    ),
-                )
+                points[h, k] = per_chunk.tile([P, CHUNK, POINTS], F32, name="points")
+                nc.sync.dma_start(points[h, k][:], v_by_half[:, h, k * CHUNK : (k + 1) * CHUNK, :])
         offsets = held.tile([P, FRUSTUMS // 16], U16, name="offsets")
         nc.sync.dma_start(offsets[:], offs)
         image = {}
-        for b in range(BLOCKS):
-            image[b] = per_block.tile([P, PLACES], F32, name="image")
-            nc.sync.dma_start(image[b][:], base[b * P : (b + 1) * P, :])
+        for h in range(HALVES):
+            image[h] = per_half.tile([P, PLACES], F32, name="image")
+            nc.sync.dma_start(image[h][:], base_by_half[:, h, :])
 
-        query, bias = {}, {}
-        for b in range(BLOCKS):
-            bias[b] = per_block.tile([P, 1], F32, name="bias")
-            nc.scalar.dma_start(bias[b][:], bv[b * P : (b + 1) * P, :])
-            query[b] = per_block.tile([P, FRUSTUMS], F32, name="query")
-            nc.scalar.dma_start(query[b][:], q[b * P : (b + 1) * P, :])
+        bias = held.tile([P, HALVES], F32, name="bias")
+        nc.scalar.dma_start(bias[:], bv.rearrange("(c2 h) o -> c2 (h o)", h=HALVES))
+        query = held.tile([P, HALVES, FRUSTUMS], F32, name="query")
+        nc.scalar.dma_start(query[:], q.rearrange("(c2 h) j -> c2 h j", h=HALVES))
 
         pooled = {}
-        for b in range(BLOCKS):
-            sums = per_block.tile([P, FRUSTUMS], F32, name="sums")
+        for h in range(HALVES):
+            sums = per_half.tile([P, FRUSTUMS], F32, name="sums")
             for k in range(CHUNKS):
-                nc.vector.tensor_reduce(sums[:, k * CHUNK : (k + 1) * CHUNK], points[b, k][:], X, ADD)
-            pooled[b] = per_block.tile([P, FRUSTUMS], F32, name="pooled")
-            nc.scalar.activation(pooled[b][:], sums[:], IDENTITY, bias=bias[b][:], scale=1.0 / POINTS)
+                nc.vector.tensor_reduce(sums[:, k * CHUNK : (k + 1) * CHUNK], points[h, k][:], X, ADD)
+            pooled[h] = per_half.tile([P, FRUSTUMS], F32, name="pooled")
+            nc.scalar.activation(pooled[h][:], sums[:], IDENTITY, bias=bias[:, h : h + 1], scale=1.0 / POINTS)
 
-        for b in range(BLOCKS):
-            nc.vector.tensor_tensor(image[b][:].indirect(offsets[:]), pooled[b][:], query[b][:], ADD)
-            nc.scalar.dma_start(out[b * P : (b + 1) * P, :], image[b][:])
+        for h in range(HALVES):
+            nc.vector.tensor_tensor(image[h][:].indirect(offsets[:]), pooled[h][:], query[:, h, :], ADD)
+            nc.scalar.dma_start(out_by_half[:, h, :], image[h][:])

@@ -9,8 +9,7 @@ X = mybir.AxisListType.X
 CHANNELS, PLACES, FRUSTUMS, POINTS = 256, 512, 128, 16
 P = 128
 HALVES = CHANNELS // P
-CHUNKS = 4
-CHUNK = FRUSTUMS // CHUNKS
+LOADS = ((64, 64), (64, 64))
 
 
 def tile_transformerfrustumencoder_kernel(tc, base, v, bv, q, offs, out):
@@ -21,13 +20,15 @@ def tile_transformerfrustumencoder_kernel(tc, base, v, bv, q, offs, out):
     with (
         tc.tile_pool(name="held", bufs=1) as held,
         tc.tile_pool(name="per_half", bufs=HALVES) as per_half,
-        tc.tile_pool(name="per_chunk", bufs=HALVES * CHUNKS) as per_chunk,
+        tc.tile_pool(name="per_load", bufs=1) as per_load,
     ):
         points = {}
         for h in range(HALVES):
-            for k in range(CHUNKS):
-                points[h, k] = per_chunk.tile([P, CHUNK, POINTS], F32, name="points")
-                nc.sync.dma_start(points[h, k][:], v_by_half[:, h, k * CHUNK : (k + 1) * CHUNK, :])
+            first = 0
+            for count in LOADS[h]:
+                points[h, first] = per_load.tile([P, count, POINTS], F32, name="points_%d_%d" % (h, first))
+                nc.sync.dma_start(points[h, first][:], v_by_half[:, h, first : first + count, :])
+                first += count
         offsets = held.tile([P, FRUSTUMS // 16], U16, name="offsets")
         nc.sync.dma_start(offsets[:], offs)
         image = {}
@@ -43,8 +44,10 @@ def tile_transformerfrustumencoder_kernel(tc, base, v, bv, q, offs, out):
         pooled = {}
         for h in range(HALVES):
             sums = per_half.tile([P, FRUSTUMS], F32, name="sums")
-            for k in range(CHUNKS):
-                nc.vector.tensor_reduce(sums[:, k * CHUNK : (k + 1) * CHUNK], points[h, k][:], X, ADD)
+            first = 0
+            for count in LOADS[h]:
+                nc.vector.tensor_reduce(sums[:, first : first + count], points[h, first][:], X, ADD)
+                first += count
             pooled[h] = per_half.tile([P, FRUSTUMS], F32, name="pooled")
             nc.scalar.activation(pooled[h][:], sums[:], IDENTITY, bias=bias[:, h : h + 1], scale=1.0 / POINTS)
 

@@ -22,6 +22,8 @@ def tile_transformerfrustumencoder_kernel(tc, base, v, bv, q, offs, out):
         tc.tile_pool(name="per_half", bufs=HALVES) as per_half,
         tc.tile_pool(name="per_load", bufs=1) as per_load,
     ):
+        bias = held.tile([P, HALVES], F32, name="bias")
+        nc.sync.dma_start(bias[:], bv.rearrange("(c2 h) o -> c2 (h o)", h=HALVES))
         points = {}
         for h in range(HALVES):
             first = 0
@@ -29,17 +31,14 @@ def tile_transformerfrustumencoder_kernel(tc, base, v, bv, q, offs, out):
                 points[h, first] = per_load.tile([P, count, POINTS], F32, name="points_%d_%d" % (h, first))
                 nc.sync.dma_start(points[h, first][:], v_by_half[:, h, first : first + count, :])
                 first += count
+        query = held.tile([P, HALVES, FRUSTUMS], F32, name="query")
+        nc.sync.dma_start(query[:], q.rearrange("(c2 h) j -> c2 h j", h=HALVES))
         offsets = held.tile([P, FRUSTUMS // 16], U16, name="offsets")
         nc.sync.dma_start(offsets[:], offs)
         image = {}
         for h in range(HALVES):
             image[h] = per_half.tile([P, PLACES], F32, name="image")
             nc.sync.dma_start(image[h][:], base_by_half[:, h, :])
-
-        bias = held.tile([P, HALVES], F32, name="bias")
-        nc.scalar.dma_start(bias[:], bv.rearrange("(c2 h) o -> c2 (h o)", h=HALVES))
-        query = held.tile([P, HALVES, FRUSTUMS], F32, name="query")
-        nc.scalar.dma_start(query[:], q.rearrange("(c2 h) j -> c2 h j", h=HALVES))
 
         pooled = {}
         for h in range(HALVES):

@@ -9,13 +9,14 @@ X = mybir.AxisListType.X
 CHANNELS, PLACES, FRUSTUMS, POINTS = 256, 512, 128, 16
 P = 128
 HALVES = CHANNELS // P
-LOADS = ((64, 64), (64, 64))
+LOADS = ((32, 32, 32, 32), (32, 32, 32, 32))
 
 
 def tile_transformerfrustumencoder_kernel(tc, base, v, bv, q, offs, out):
     nc = tc.nc
     base_by_half = base.rearrange("(c2 h) s -> c2 h s", h=HALVES)
     out_by_half = out.rearrange("(c2 h) s -> c2 h s", h=HALVES)
+    q_by_half = q.rearrange("(c2 h) j -> c2 h j", h=HALVES)
     v_by_half = v.rearrange("(c2 h) (j p) -> c2 h j p", h=HALVES, p=POINTS)
     with (
         tc.tile_pool(name="held", bufs=1) as held,
@@ -31,12 +32,12 @@ def tile_transformerfrustumencoder_kernel(tc, base, v, bv, q, offs, out):
                 points[h, first] = per_load.tile([P, count, POINTS], F32, name="points_%d_%d" % (h, first))
                 nc.sync.dma_start(points[h, first][:], v_by_half[:, h, first : first + count, :])
                 first += count
-        query = held.tile([P, HALVES, FRUSTUMS], F32, name="query")
-        nc.sync.dma_start(query[:], q.rearrange("(c2 h) j -> c2 h j", h=HALVES))
         offsets = held.tile([P, FRUSTUMS // 16], U16, name="offsets")
         nc.sync.dma_start(offsets[:], offs)
-        image = {}
+        query, image = {}, {}
         for h in range(HALVES):
+            query[h] = per_half.tile([P, FRUSTUMS], F32, name="query")
+            nc.sync.dma_start(query[h][:], q_by_half[:, h, :])
             image[h] = per_half.tile([P, PLACES], F32, name="image")
             nc.sync.dma_start(image[h][:], base_by_half[:, h, :])
 
@@ -51,5 +52,5 @@ def tile_transformerfrustumencoder_kernel(tc, base, v, bv, q, offs, out):
             nc.scalar.activation(pooled[h][:], sums[:], IDENTITY, bias=bias[:, h : h + 1], scale=1.0 / POINTS)
 
         for h in range(HALVES):
-            nc.vector.tensor_tensor(image[h][:].indirect(offsets[:]), pooled[h][:], query[:, h, :], ADD)
+            nc.vector.tensor_tensor(image[h][:].indirect(offsets[:]), pooled[h][:], query[h][:], ADD)
             nc.scalar.dma_start(out_by_half[:, h, :], image[h][:])

@@ -3,7 +3,7 @@ import concourse.mybir as mybir
 F32 = mybir.dt.float32
 U16 = mybir.dt.uint16
 ADD = mybir.AluOpType.add
-IDENTITY = mybir.ActivationFunctionType.Identity
+MULT = mybir.AluOpType.mult
 X = mybir.AxisListType.X
 
 CHANNELS, PLACES, FRUSTUMS, POINTS = 256, 512, 128, 16
@@ -23,8 +23,6 @@ def tile_transformerfrustumencoder_kernel(tc, base, v, bv, q, offs, out):
         tc.tile_pool(name="per_half", bufs=HALVES) as per_half,
         tc.tile_pool(name="per_load", bufs=1) as per_load,
     ):
-        bias = held.tile([P, HALVES], F32, name="bias")
-        nc.sync.dma_start(bias[:], bv.rearrange("(c2 h) o -> c2 (h o)", h=HALVES))
         points = {}
         for h in range(HALVES):
             first = 0
@@ -32,6 +30,8 @@ def tile_transformerfrustumencoder_kernel(tc, base, v, bv, q, offs, out):
                 points[h, first] = per_load.tile([P, count, POINTS], F32, name="points_%d_%d" % (h, first))
                 nc.sync.dma_start(points[h, first][:], v_by_half[:, h, first : first + count, :])
                 first += count
+        bias = held.tile([P, HALVES], F32, name="bias")
+        nc.sync.dma_start(bias[:], bv.rearrange("(c2 h) o -> c2 (h o)", h=HALVES))
         offsets = held.tile([P, FRUSTUMS // 16], U16, name="offsets")
         nc.sync.dma_start(offsets[:], offs)
         query, image = {}, {}
@@ -41,16 +41,15 @@ def tile_transformerfrustumencoder_kernel(tc, base, v, bv, q, offs, out):
             image[h] = per_half.tile([P, PLACES], F32, name="image")
             nc.sync.dma_start(image[h][:], base_by_half[:, h, :])
 
-        pooled = {}
+        sums = {}
         for h in range(HALVES):
-            sums = per_half.tile([P, FRUSTUMS], F32, name="sums")
+            sums[h] = per_half.tile([P, FRUSTUMS], F32, name="sums")
             first = 0
             for count in LOADS[h]:
-                nc.vector.tensor_reduce(sums[:, first : first + count], points[h, first][:], X, ADD)
+                nc.vector.tensor_reduce(sums[h][:, first : first + count], points[h, first][:], X, ADD)
                 first += count
-            pooled[h] = per_half.tile([P, FRUSTUMS], F32, name="pooled")
-            nc.scalar.activation(pooled[h][:], sums[:], IDENTITY, bias=bias[:, h : h + 1], scale=1.0 / POINTS)
-
         for h in range(HALVES):
-            nc.vector.tensor_tensor(image[h][:].indirect(offsets[:]), pooled[h][:], query[h][:], ADD)
-            nc.scalar.dma_start(out_by_half[:, h, :], image[h][:])
+            pooled = per_half.tile([P, FRUSTUMS], F32, name="pooled")
+            nc.vector.tensor_scalar(pooled[:], sums[h][:], 1.0 / POINTS, bias[:, h : h + 1], op0=MULT, op1=ADD)
+            nc.vector.tensor_tensor(image[h][:].indirect(offsets[:]), pooled[:], query[h][:], ADD)
+            nc.sync.dma_start(out_by_half[:, h, :], image[h][:])

import concourse.mybir as mybir

F32 = mybir.dt.float32
U16 = mybir.dt.uint16
ADD = mybir.AluOpType.add
MULT = mybir.AluOpType.mult
X = mybir.AxisListType.X

CHANNELS, PLACES, FRUSTUMS, POINTS = 256, 512, 128, 16
P = 128
HALVES = CHANNELS // P
LOADS = ((32, 32, 32, 32), (32, 32, 32, 32))


def tile_transformerfrustumencoder_kernel(tc, base, v, bv, q, offs, out):
    nc = tc.nc
    base_by_half = base.rearrange("(c2 h) s -> c2 h s", h=HALVES)
    out_by_half = out.rearrange("(c2 h) s -> c2 h s", h=HALVES)
    q_by_half = q.rearrange("(c2 h) j -> c2 h j", h=HALVES)
    v_by_half = v.rearrange("(c2 h) (j p) -> c2 h j p", h=HALVES, p=POINTS)
    with (
        tc.tile_pool(name="held", bufs=1) as held,
        tc.tile_pool(name="per_half", bufs=HALVES) as per_half,
        tc.tile_pool(name="per_load", bufs=1) as per_load,
    ):
        points = {}
        for h in range(HALVES):
            first = 0
            for count in LOADS[h]:
                points[h, first] = per_load.tile([P, count, POINTS], F32, name="points_%d_%d" % (h, first))
                nc.sync.dma_start(points[h, first][:], v_by_half[:, h, first : first + count, :])
                first += count
        bias = held.tile([P, HALVES], F32, name="bias")
        nc.sync.dma_start(bias[:], bv.rearrange("(c2 h) o -> c2 (h o)", h=HALVES))
        offsets = held.tile([P, FRUSTUMS // 16], U16, name="offsets")
        nc.sync.dma_start(offsets[:], offs)
        query, image = {}, {}
        for h in range(HALVES):
            query[h] = per_half.tile([P, FRUSTUMS], F32, name="query")
            nc.sync.dma_start(query[h][:], q_by_half[:, h, :])
            image[h] = per_half.tile([P, PLACES], F32, name="image")
            nc.sync.dma_start(image[h][:], base_by_half[:, h, :])

        sums = {}
        for h in range(HALVES):
            sums[h] = per_half.tile([P, FRUSTUMS], F32, name="sums")
            first = 0
            for count in LOADS[h]:
                nc.vector.tensor_reduce(sums[h][:, first : first + count], points[h, first][:], X, ADD)
                first += count
        for h in range(HALVES):
            pooled = per_half.tile([P, FRUSTUMS], F32, name="pooled")
            nc.vector.tensor_scalar(pooled[:], sums[h][:], 1.0 / POINTS, bias[:, h : h + 1], op0=MULT, op1=ADD)
            nc.vector.tensor_tensor(image[h][:].indirect(offsets[:]), pooled[:], query[h][:], ADD)
            nc.sync.dma_start(out_by_half[:, h, :], image[h][:])
